import numpy as np
import ml_dtypes


def mxq(x, axis, fmt="e4m3"):
    dtype, down = {"e4m3": (ml_dtypes.float8_e4m3fn, 7), "e5m2": (ml_dtypes.float8_e5m2, 14)}[fmt]
    v = np.moveaxis(np.asarray(x, np.float32).astype(ml_dtypes.bfloat16).astype(np.float64), axis, -1)
    blocks = v.reshape(v.shape[:-1] + (-1, 32))
    amax = np.abs(blocks).max(-1, keepdims=True)
    byte = np.maximum(np.where(amax > 0, np.frexp(amax)[1] - 1 + 127, 0) - down, 1)
    scale = np.exp2(byte - 127.0)
    codes = (blocks / scale).astype(np.float32).astype(dtype).astype(np.float64)
    return np.moveaxis((codes * scale).reshape(v.shape), -1, axis)


WIDE = False


def mx_kscale(k):
    if not WIDE:
        return np.ones(k)
    levels = np.array([10, -10, 5, -5, 0])
    a = np.random.permutation(np.resize(levels, k // 512 * 4)).reshape(k // 512, 4)
    idx = np.arange(k)
    return np.exp2(a[idx // 512, idx % 128 // 32])


BF16 = ml_dtypes.bfloat16


def bf(x):
    return np.asarray(x, np.float32).astype(BF16)


def f64(x):
    return np.asarray(x).astype(np.float64)


B, S, D, H, KV, DH, QB = 1, 1024, 1024, 16, 4, 128, 512
HALF = DH // 2
EPS = 1e-6


def rope_tables():
    inv_freq = 1.0 / (10000.0 ** (np.arange(HALF) / HALF))
    ang = np.arange(S)[:, None] * inv_freq[None, :]
    ang = np.concatenate([ang, ang], axis=-1)
    return np.sin(ang), np.cos(ang)


def rmsnorm(u, scale, shift):
    rms = np.sqrt(np.mean(u * u, axis=-1, keepdims=True) + EPS)
    return u / rms * (1.0 + scale) + shift


def apply_rope(u, sin, cos):
    rot = np.concatenate([-u[..., HALF:], u[..., :HALF]], axis=-1)
    return u * cos[None, None, :S, :] + rot * sin[None, None, :S, :]


def heads(u, n):
    return u.reshape(B, S, n, DH).transpose(0, 2, 1, 3)


def setup_inputs():
    s = mx_kscale(D)
    sin, cos = rope_tables()
    return {"x": bf(np.random.standard_normal((B, S, D)) * s),
            "sin_thetas": bf(sin), "cos_thetas": bf(cos),
            "wq": bf(np.random.standard_normal((H * DH, D)) / np.sqrt(D) / s),
            "wk": bf(np.random.standard_normal((KV * DH, D)) / np.sqrt(D) / s),
            "wv": bf(np.random.standard_normal((KV * DH, D)) * 2.0 / np.sqrt(D) / s),
            "q_scale": bf(np.random.standard_normal(DH) * 0.1), "q_shift": bf(np.random.standard_normal(DH) * 0.1),
            "k_scale": bf(np.random.standard_normal(DH) * 0.1), "k_shift": bf(np.random.standard_normal(DH) * 0.1)}


def reference(x, sin_thetas, cos_thetas, wq, wk, wv, q_scale, q_shift, k_scale, k_shift):
    xq = mxq(f64(x), 2, "e4m3")
    q = heads(xq @ mxq(f64(wq), 1, "e4m3").T, H)
    k = heads(xq @ mxq(f64(wk), 1, "e4m3").T, KV)
    v = heads(xq @ mxq(f64(wv), 1, "e4m3").T, KV)
    q = rmsnorm(q, f64(q_scale), f64(q_shift))
    k = rmsnorm(k, f64(k_scale), f64(k_shift))
    q = apply_rope(q, f64(sin_thetas), f64(cos_thetas))
    k = apply_rope(k, f64(sin_thetas), f64(cos_thetas))
    return q, k, v

@@ -1,0 +1,241 @@
+from contextlib import ExitStack
+
+import concourse.mybir as mybir
+from concourse.masks import make_identity
+
+F32 = mybir.dt.float32
+BF16 = mybir.dt.bfloat16
+U32 = mybir.dt.uint32
+U8 = mybir.dt.uint8
+FP8X4 = mybir.dt.float8_e4m3fn_x4
+ALU = mybir.AluOpType
+ACT = mybir.ActivationFunctionType
+
+P = 128
+S = 1024
+D = 1024
+DH = 128
+HALF = DH // 2
+EPS = 1e-6
+TILES = S // P
+PACK = 4
+PASSES = D // (P * PACK)
+CHUNKS = D // 2 // P
+HEADS = 4
+COLS = HEADS * DH
+PAIR = 2
+
+FLOPS = 2 * S * D * (16 + 4 + 4) * DH
+
+
+def tile_groupqueryattention_pa_kernel(
+    tc, x, sin_thetas, cos_thetas, wq, wk, wv, q_scale, q_shift, k_scale, k_shift, out_0, out_1, out_2
+):
+    nc = tc.nc
+    with ExitStack() as ctx:
+        keep = ctx.enter_context(tc.tile_pool(name="keep", bufs=1))
+        grouped_pool = ctx.enter_context(tc.tile_pool(name="grouped", bufs=2))
+        weight_pool = ctx.enter_context(tc.tile_pool(name="weights", bufs=2))
+        product_pool = ctx.enter_context(tc.tile_pool(name="products", bufs=3))
+        stage_pool = ctx.enter_context(tc.tile_pool(name="stage", bufs=4))
+        small_pool = ctx.enter_context(tc.tile_pool(name="small", bufs=4))
+        flip_psum = ctx.enter_context(tc.psum_pool(name="flip", bufs=4))
+        acc_psum = ctx.enter_context(tc.psum_pool(name="acc", bufs=4))
+
+        groups = [(wq[COLS * g : COLS * (g + 1), :], out_0[0, HEADS * g : HEADS * (g + 1)], 0) for g in range(4)]
+        groups.append((wk, out_1[0], 1))
+        groups.append((wv, out_2[0], None))
+
+        cos_sb = keep.tile([P, TILES, DH], BF16)
+        sin_sb = keep.tile([P, TILES, DH], BF16)
+        nc.scalar.dma_start(out=cos_sb[:], in_=cos_thetas.rearrange("(p t) d -> p t d", t=TILES))
+        nc.scalar.dma_start(out=sin_sb[:], in_=sin_thetas.rearrange("(p t) d -> p t d", t=TILES))
+        vectors = keep.tile([P, 4, DH], BF16)
+        nc.vector.memset(vectors[:], 0.0)
+        for j, vector in enumerate((q_scale, k_scale, q_shift, k_shift)):
+            nc.scalar.dma_start(out=vectors[0:1, j, :], in_=vector.unsqueeze(0))
+
+        x_sb = keep.tile([P, TILES, D], BF16)
+        x_view = x[0].rearrange("(p t) d -> p t d", t=TILES)
+        w_sb = [keep.tile([P, HEADS, D], BF16, name="w_sb%d" % g) for g in range(len(groups))]
+
+        def load_x(pair):
+            tiles = slice(PAIR * pair, PAIR * (pair + 1))
+            nc.sync.dma_start(out=x_sb[:, tiles, :], in_=x_view[:, tiles, :])
+
+        def load_w(g):
+            nc.sync.dma_start(out=w_sb[g][:], in_=groups[g][0].rearrange("(r p) i -> p r i", p=P))
+
+        load_x(0)
+        load_w(0)
+        for pair in range(1, TILES // PAIR):
+            load_x(pair)
+        for g in range(1, len(groups)):
+            load_w(g)
+
+        ident = keep.tile([P, P], F32)
+        make_identity(nc, ident[:])
+        ones = keep.tile([P, P], BF16)
+        nc.vector.memset(ones[:], 1.0)
+        eps = keep.tile([P, 1], F32)
+        nc.vector.memset(eps[:], EPS)
+
+        spread = flip_psum.tile([P, 4, DH], F32, tag="flip")
+        nc.tensor.matmul(
+            out=spread[:].rearrange("p j d -> p (j d)"),
+            lhsT=ones[:],
+            rhs=vectors[:].rearrange("p j d -> p (j d)"),
+            start=True,
+            stop=True,
+        )
+        gain = keep.tile([P, 2, DH], F32)
+        shift = keep.tile([P, 2, DH], F32)
+        nc.vector.tensor_scalar_add(out=gain[:], in0=spread[:, 0:2, :], scalar1=1.0)
+        nc.vector.tensor_copy(out=shift[:], in_=spread[:, 2:4, :])
+
+        cos_sin = keep.tile([P, TILES, 2, DH], F32)
+        nc.vector.tensor_copy(out=cos_sin[:, :, 0, :], in_=cos_sb[:])
+        nc.vector.tensor_copy(out=cos_sin[:, :, 1, 0:HALF], in_=sin_sb[:, :, HALF:DH])
+        nc.vector.tensor_scalar_mul(out=cos_sin[:, :, 1, HALF:DH], in0=sin_sb[:, :, 0:HALF], scalar1=-1.0)
+
+        def make_tables(engine, which):
+            both = cos_sin[:].rearrange("p t j d -> p (t j) d")
+            factors = keep.tile([P, TILES, 2, DH], F32, name="factors%d" % which)
+            engine.tensor_tensor(
+                out=factors[:].rearrange("p t j d -> p (t j) d"),
+                in0=both,
+                in1=gain[:, which, :].unsqueeze(1).to_broadcast([P, TILES * 2, DH]),
+                op=ALU.mult,
+            )
+            shifted = keep.tile([P, TILES, 2, DH], F32, name="shifted%d" % which, tag="shifted")
+            engine.tensor_tensor(
+                out=shifted[:].rearrange("p t j d -> p (t j) d"),
+                in0=both,
+                in1=shift[:, which, :].unsqueeze(1).to_broadcast([P, TILES * 2, DH]),
+                op=ALU.mult,
+            )
+            offset = keep.tile([P, TILES, DH], F32, name="offset%d" % which)
+            engine.tensor_tensor(
+                out=offset[:, :, 0:HALF], in0=shifted[:, :, 0, 0:HALF], in1=shifted[:, :, 1, HALF:DH], op=ALU.add
+            )
+            engine.tensor_tensor(
+                out=offset[:, :, HALF:DH], in0=shifted[:, :, 0, HALF:DH], in1=shifted[:, :, 1, 0:HALF], op=ALU.add
+            )
+            return factors, offset
+
+        tables = [make_tables(nc.vector, 0), make_tables(nc.gpsimd, 1)]
+
+        def flip_rows(rows, grouped_words):
+            words = rows.bitcast(F32)
+            flipped = flip_psum.tile([P, CHUNKS, P], F32, tag="flip")
+            for piece in range(CHUNKS):
+                nc.tensor.transpose(flipped[:, piece, :], words[:, P * piece : P * (piece + 1)], ident[:])
+            nc.scalar.copy(out=grouped_words, in_=flipped[:].rearrange("p (c u) n -> p c n u", u=2))
+
+        x_codes = keep.tile([P, TILES, PASSES, P], U32, align_bytes=64)
+        x_scales = keep.tile([P, TILES, PASSES, P], U8, align_bytes=64)
+
+        def quantise_x(pair):
+            x_grouped = grouped_pool.tile([P, PAIR, PASSES, P, PACK], BF16, align_bytes=64)
+            for i in range(PAIR):
+                flip_rows(x_sb[:, PAIR * pair + i, :], x_grouped[:, i].bitcast(F32))
+            tiles = slice(PAIR * pair, PAIR * (pair + 1))
+            nc.vector.quantize_mx(
+                out=x_codes[:, tiles].rearrange("p t c m -> p (t c m)").bitcast(FP8X4),
+                scales=x_scales[:, tiles].rearrange("p t c m -> p (t c m)"),
+                in_=x_grouped[:].rearrange("p t c m j -> p (t c m j)"),
+            )
+
+        def quantise_w(g):
+            w_grouped = grouped_pool.tile([P, PASSES, COLS, PACK], BF16, align_bytes=64)
+            for r in range(HEADS):
+                flip_rows(w_sb[g][:, r, :], w_grouped[:, :, DH * r : DH * (r + 1), :].bitcast(F32))
+            w_codes = weight_pool.tile([P, PASSES, COLS], U32, align_bytes=64)
+            w_scales = weight_pool.tile([P, PASSES, COLS], U8, align_bytes=64)
+            nc.vector.quantize_mx(
+                out=w_codes[:].rearrange("p c n -> p (c n)").bitcast(FP8X4),
+                scales=w_scales[:].rearrange("p c n -> p (c n)"),
+                in_=w_grouped[:].rearrange("p c n j -> p (c n j)"),
+            )
+            return w_codes, w_scales
+
+        def project(t, w_codes, w_scales):
+            acc = acc_psum.tile([P, COLS], F32)
+            for c in range(PASSES):
+                nc.tensor.matmul_mx(
+                    out=acc[:],
+                    lhsT=x_codes[:, t, c, :].bitcast(FP8X4),
+                    lhsT_scale=x_scales[:, t, c, :],
+                    rhs=w_codes[:, c, :].bitcast(FP8X4),
+                    rhs_scale=w_scales[:, c, :],
+                    start=(c == 0),
+                    stop=(c == PASSES - 1),
+                )
+            return acc
+
+        squares = keep.tile([P, DH], F32)
+
+        def norm_and_rope(first, weights, stage, which):
+            factors, offset = tables[which]
+            products = product_pool.tile([P, PAIR, 2, COLS], F32)
+            sum_sq = small_pool.tile([P, PAIR * HEADS], F32)
+            for i in range(PAIR):
+                acc = project(first + i, *weights)
+                for h in range(HEADS):
+                    nc.scalar.activation(
+                        out=squares[:],
+                        in_=acc[:, DH * h : DH * (h + 1)],
+                        func=ACT.Square,
+                        accum_out=sum_sq[:, HEADS * i + h : HEADS * i + h + 1],
+                    )
+                nc.vector.tensor_tensor(
+                    out=products[:, i].rearrange("p j (h d) -> p j h d", d=DH),
+                    in0=acc[:].rearrange("p (h d) -> p h d", d=DH).unsqueeze(1).to_broadcast([P, 2, HEADS, DH]),
+                    in1=factors[:, first + i].unsqueeze(2).to_broadcast([P, 2, HEADS, DH]),
+                    op=ALU.mult,
+                )
+            rms = small_pool.tile([P, PAIR * HEADS], F32)
+            nc.scalar.activation(out=rms[:], in_=sum_sq[:], func=ACT.Sqrt, scale=1.0 / DH, bias=eps[:, 0:1])
+            r = small_pool.tile([P, PAIR * HEADS], F32)
+            nc.vector.reciprocal(out=r[:], in_=rms[:])
+            straight = products[:, :, 0, :].rearrange("p i (h d) -> p i h d", d=DH)
+            crossed = products[:, :, 1, :].rearrange("p i (h d) -> p i h d", d=DH)
+            rotated = stage[:].rearrange("p h i d -> p i h d")
+            nc.gpsimd.tensor_tensor(
+                out=rotated[:, :, :, 0:HALF], in0=straight[:, :, :, 0:HALF], in1=crossed[:, :, :, HALF:DH], op=ALU.add
+            )
+            nc.gpsimd.tensor_tensor(
+                out=rotated[:, :, :, HALF:DH], in0=straight[:, :, :, HALF:DH], in1=crossed[:, :, :, 0:HALF], op=ALU.add
+            )
+            for i in range(PAIR):
+                for h in range(HEADS):
+                    nc.vector.scalar_tensor_tensor(
+                        out=stage[:, h, i, :],
+                        in0=stage[:, h, i, :],
+                        scalar=r[:, HEADS * i + h : HEADS * i + h + 1],
+                        in1=offset[:, first + i, :],
+                        op0=ALU.mult,
+                        op1=ALU.add,
+                    )
+
+        def copy_out(first, weights, stage):
+            for i in range(PAIR):
+                acc = project(first + i, *weights)
+                nc.scalar.copy(out=stage[:, :, i, :], in_=acc[:].rearrange("p (h d) -> p h d", d=DH))
+
+        quantise_x(0)
+        weights = quantise_w(0)
+        for pair in range(1, TILES // PAIR):
+            quantise_x(pair)
+        for g in range(len(groups)):
+            out, which = groups[g][1], groups[g][2]
+            following = quantise_w(g + 1) if g + 1 < len(groups) else None
+            out_view = out.rearrange("h (p t) d -> p h t d", t=TILES)
+            for first in range(0, TILES, PAIR):
+                stage = stage_pool.tile([P, HEADS, PAIR, DH], F32)
+                if which is None:
+                    copy_out(first, weights, stage)
+                else:
+                    norm_and_rope(first, weights, stage, which)
+                nc.sync.dma_start(out=out_view[:, :, first : first + PAIR, :], in_=stage[:])
+            weights = following

@@ -24,6 +24,8 @@ CHUNKS = D // 2 // P
 HEADS = 4
 COLS = HEADS * DH
 PAIR = 2
+ROUNDS_PER_GROUP = TILES // PAIR
+LEAD = 2
 
 FLOPS = 2 * S * D * (16 + 4 + 4) * DH
 
@@ -41,10 +43,12 @@ def tile_groupqueryattention_pa_kernel(
         small_pool = ctx.enter_context(tc.tile_pool(name="small", bufs=4))
         flip_psum = ctx.enter_context(tc.psum_pool(name="flip", bufs=4))
         acc_psum = ctx.enter_context(tc.psum_pool(name="acc", bufs=4))
+        ctx.enter_context(tc.manual_schedule())
 
         groups = [(wq[COLS * g : COLS * (g + 1), :], out_0[0, HEADS * g : HEADS * (g + 1)], 0) for g in range(4)]
         groups.append((wk, out_1[0], 1))
         groups.append((wv, out_2[0], None))
+        rounds = len(groups) * ROUNDS_PER_GROUP
 
         cos_sb = keep.tile([P, TILES, DH], BF16)
         sin_sb = keep.tile([P, TILES, DH], BF16)
@@ -68,7 +72,7 @@ def tile_groupqueryattention_pa_kernel(
 
         load_x(0)
         load_w(0)
-        for pair in range(1, TILES // PAIR):
+        for pair in range(1, ROUNDS_PER_GROUP):
             load_x(pair)
         for g in range(1, len(groups)):
             load_w(g)
@@ -88,42 +92,39 @@ def tile_groupqueryattention_pa_kernel(
             start=True,
             stop=True,
         )
+        low, high = slice(0, HALF), slice(HALF, DH)
         gain = keep.tile([P, 2, DH], F32)
+        gain_s = keep.tile([P, 2, DH], F32)
         shift = keep.tile([P, 2, DH], F32)
+        shift_r = keep.tile([P, 2, DH], F32)
         nc.vector.tensor_scalar_add(out=gain[:], in0=spread[:, 0:2, :], scalar1=1.0)
+        nc.vector.tensor_copy(out=gain_s[:, :, low], in_=gain[:, :, low])
+        nc.vector.tensor_scalar_mul(out=gain_s[:, :, high], in0=gain[:, :, high], scalar1=-1.0)
         nc.vector.tensor_copy(out=shift[:], in_=spread[:, 2:4, :])
+        nc.vector.tensor_scalar_mul(out=shift_r[:, :, low], in0=spread[:, 2:4, high], scalar1=-1.0)
+        nc.vector.tensor_copy(out=shift_r[:, :, high], in_=spread[:, 2:4, low])
 
-        cos_sin = keep.tile([P, TILES, 2, DH], F32)
-        nc.vector.tensor_copy(out=cos_sin[:, :, 0, :], in_=cos_sb[:])
-        nc.vector.tensor_copy(out=cos_sin[:, :, 1, 0:HALF], in_=sin_sb[:, :, HALF:DH])
-        nc.vector.tensor_scalar_mul(out=cos_sin[:, :, 1, HALF:DH], in0=sin_sb[:, :, 0:HALF], scalar1=-1.0)
+        def over_tiles(vector, width):
+            return vector.unsqueeze(1).to_broadcast([P, TILES, width])
 
-        def make_tables(engine, which):
-            both = cos_sin[:].rearrange("p t j d -> p (t j) d")
+        def make_factors(engine, which):
             factors = keep.tile([P, TILES, 2, DH], F32, name="factors%d" % which)
+            engine.tensor_tensor(out=factors[:, :, 0, :], in0=cos_sb[:], in1=over_tiles(gain[:, which, :], DH), op=ALU.mult)
             engine.tensor_tensor(
-                out=factors[:].rearrange("p t j d -> p (t j) d"),
-                in0=both,
-                in1=gain[:, which, :].unsqueeze(1).to_broadcast([P, TILES * 2, DH]),
-                op=ALU.mult,
-            )
-            shifted = keep.tile([P, TILES, 2, DH], F32, name="shifted%d" % which, tag="shifted")
-            engine.tensor_tensor(
-                out=shifted[:].rearrange("p t j d -> p (t j) d"),
-                in0=both,
-                in1=shift[:, which, :].unsqueeze(1).to_broadcast([P, TILES * 2, DH]),
-                op=ALU.mult,
-            )
-            offset = keep.tile([P, TILES, DH], F32, name="offset%d" % which)
-            engine.tensor_tensor(
-                out=offset[:, :, 0:HALF], in0=shifted[:, :, 0, 0:HALF], in1=shifted[:, :, 1, HALF:DH], op=ALU.add
+                out=factors[:, :, 1, low], in0=sin_sb[:, :, high], in1=over_tiles(gain_s[:, which, low], HALF), op=ALU.mult
             )
             engine.tensor_tensor(
-                out=offset[:, :, HALF:DH], in0=shifted[:, :, 0, HALF:DH], in1=shifted[:, :, 1, 0:HALF], op=ALU.add
+                out=factors[:, :, 1, high], in0=sin_sb[:, :, low], in1=over_tiles(gain_s[:, which, high], HALF), op=ALU.mult
             )
-            return factors, offset
+            return factors
 
-        tables = [make_tables(nc.vector, 0), make_tables(nc.gpsimd, 1)]
+        def make_offset(engine, which):
+            offset = keep.tile([P, TILES, DH], F32, name="offset%d" % which)
+            turned = keep.tile([P, TILES, DH], F32, name="turned%d" % which)
+            engine.tensor_tensor(out=offset[:], in0=cos_sb[:], in1=over_tiles(shift[:, which, :], DH), op=ALU.mult)
+            engine.tensor_tensor(out=turned[:], in0=sin_sb[:], in1=over_tiles(shift_r[:, which, :], DH), op=ALU.mult)
+            engine.tensor_tensor(out=offset[:], in0=offset[:], in1=turned[:], op=ALU.add)
+            return offset
 
         def flip_rows(rows, grouped_words):
             words = rows.bitcast(F32)
@@ -159,6 +160,15 @@ def tile_groupqueryattention_pa_kernel(
             )
             return w_codes, w_scales
 
+        weights = {}
+
+        def prepare(n):
+            g, pair = divmod(n, ROUNDS_PER_GROUP)
+            if g == 0:
+                quantise_x(pair)
+            if pair == 0 and g < len(groups):
+                weights[g] = quantise_w(g)
+
         def project(t, w_codes, w_scales):
             acc = acc_psum.tile([P, COLS], F32)
             for c in range(PASSES):
@@ -175,12 +185,11 @@ def tile_groupqueryattention_pa_kernel(
 
         squares = keep.tile([P, DH], F32)
 
-        def norm_and_rope(first, weights, stage, which):
-            factors, offset = tables[which]
+        def rotate(first, w_pair, factors, stage):
             products = product_pool.tile([P, PAIR, 2, COLS], F32)
             sum_sq = small_pool.tile([P, PAIR * HEADS], F32)
             for i in range(PAIR):
-                acc = project(first + i, *weights)
+                acc = project(first + i, *w_pair)
                 for h in range(HEADS):
                     nc.scalar.activation(
                         out=squares[:],
@@ -202,11 +211,14 @@ def tile_groupqueryattention_pa_kernel(
             crossed = products[:, :, 1, :].rearrange("p i (h d) -> p i h d", d=DH)
             rotated = stage[:].rearrange("p h i d -> p i h d")
             nc.gpsimd.tensor_tensor(
-                out=rotated[:, :, :, 0:HALF], in0=straight[:, :, :, 0:HALF], in1=crossed[:, :, :, HALF:DH], op=ALU.add
+                out=rotated[:, :, :, low], in0=straight[:, :, :, low], in1=crossed[:, :, :, high], op=ALU.add
             )
             nc.gpsimd.tensor_tensor(
-                out=rotated[:, :, :, HALF:DH], in0=straight[:, :, :, HALF:DH], in1=crossed[:, :, :, 0:HALF], op=ALU.add
+                out=rotated[:, :, :, high], in0=straight[:, :, :, high], in1=crossed[:, :, :, low], op=ALU.add
             )
+            return r
+
+        def finish(first, stage, r, offset, out_rows):
             for i in range(PAIR):
                 for h in range(HEADS):
                     nc.vector.scalar_tensor_tensor(
@@ -217,25 +229,32 @@ def tile_groupqueryattention_pa_kernel(
                         op0=ALU.mult,
                         op1=ALU.add,
                     )
+            nc.sync.dma_start(out=out_rows, in_=stage[:])
 
-        def copy_out(first, weights, stage):
-            for i in range(PAIR):
-                acc = project(first + i, *weights)
-                nc.scalar.copy(out=stage[:, :, i, :], in_=acc[:].rearrange("p (h d) -> p h d", d=DH))
-
+        factors = [make_factors(nc.vector, 0), make_factors(nc.vector, 1)]
+        offsets = [make_offset(nc.gpsimd, 0)]
         quantise_x(0)
-        weights = quantise_w(0)
-        for pair in range(1, TILES // PAIR):
-            quantise_x(pair)
-        for g in range(len(groups)):
-            out, which = groups[g][1], groups[g][2]
-            following = quantise_w(g + 1) if g + 1 < len(groups) else None
-            out_view = out.rearrange("h (p t) d -> p h t d", t=TILES)
-            for first in range(0, TILES, PAIR):
-                stage = stage_pool.tile([P, HEADS, PAIR, DH], F32)
-                if which is None:
-                    copy_out(first, weights, stage)
-                else:
-                    norm_and_rope(first, weights, stage, which)
-                nc.sync.dma_start(out=out_view[:, :, first : first + PAIR, :], in_=stage[:])
-            weights = following
+        offsets.append(make_offset(nc.vector, 1))
+        weights[0] = quantise_w(0)
+        quantise_x(1)
+
+        waiting = None
+        for n in range(rounds):
+            g, pair = divmod(n, ROUNDS_PER_GROUP)
+            first = PAIR * pair
+            which = groups[g][2]
+            out_rows = groups[g][1].rearrange("h (p t) d -> p h t d", t=TILES)[:, :, first : first + PAIR, :]
+            stage = stage_pool.tile([P, HEADS, PAIR, DH], F32)
+            if which is None:
+                for i in range(PAIR):
+                    acc = project(first + i, *weights[g])
+                    nc.scalar.copy(out=stage[:, :, i, :], in_=acc[:].rearrange("p (h d) -> p h d", d=DH))
+                nc.sync.dma_start(out=out_rows, in_=stage[:])
+                begun = None
+            else:
+                r = rotate(first, weights[g], factors[which], stage)
+                begun = (first, stage, r, offsets[which], out_rows)
+            prepare(n + LEAD)
+            if waiting is not None:
+                finish(*waiting)
+            waiting = begun

@@ -25,6 +25,7 @@ HEADS = 4
 COLS = HEADS * DH
 PAIR = 2
 ROUNDS_PER_GROUP = TILES // PAIR
+BANK_TILES = 512 // DH
 LEAD = 2
 
 FLOPS = 2 * S * D * (16 + 4 + 4) * DH
@@ -41,7 +42,8 @@ def tile_groupqueryattention_pa_kernel(
         product_pool = ctx.enter_context(tc.tile_pool(name="products", bufs=3))
         stage_pool = ctx.enter_context(tc.tile_pool(name="stage", bufs=4))
         small_pool = ctx.enter_context(tc.tile_pool(name="small", bufs=4))
-        flip_psum = ctx.enter_context(tc.psum_pool(name="flip", bufs=4))
+        flip_psum = ctx.enter_context(tc.psum_pool(name="flip", bufs=2))
+        offset_psum = ctx.enter_context(tc.psum_pool(name="offset", bufs=2))
         acc_psum = ctx.enter_context(tc.psum_pool(name="acc", bufs=4))
         ctx.enter_context(tc.manual_schedule())
 
@@ -118,12 +120,25 @@ def tile_groupqueryattention_pa_kernel(
             )
             return factors
 
+        offset_sb = keep.tile([P, 2, TILES, DH], F32)
+
         def make_offset(engine, which):
-            offset = keep.tile([P, TILES, DH], F32, name="offset%d" % which)
             turned = keep.tile([P, TILES, DH], F32, name="turned%d" % which)
-            engine.tensor_tensor(out=offset[:], in0=cos_sb[:], in1=over_tiles(shift[:, which, :], DH), op=ALU.mult)
+            engine.tensor_tensor(
+                out=offset_sb[:, which], in0=cos_sb[:], in1=over_tiles(shift[:, which, :], DH), op=ALU.mult
+            )
             engine.tensor_tensor(out=turned[:], in0=sin_sb[:], in1=over_tiles(shift_r[:, which, :], DH), op=ALU.mult)
-            engine.tensor_tensor(out=offset[:], in0=offset[:], in1=turned[:], op=ALU.add)
+            engine.tensor_tensor(out=offset_sb[:, which], in0=offset_sb[:, which], in1=turned[:], op=ALU.add)
+
+        def offsets_into_psum(which, part):
+            offset = offset_psum.tile([P, BANK_TILES, DH], F32)
+            nc.tensor.matmul(
+                out=offset[:].rearrange("p t d -> p (t d)"),
+                lhsT=ident[:],
+                rhs=offset_sb[:, which, BANK_TILES * part : BANK_TILES * (part + 1), :].rearrange("p t d -> p (t d)"),
+                start=True,
+                stop=True,
+            )
             return offset
 
         def flip_rows(rows, grouped_words):
@@ -218,23 +233,29 @@ def tile_groupqueryattention_pa_kernel(
             )
             return r
 
-        def finish(first, stage, r, offset, out_rows):
+        offsets = {}
+
+        def finish(first, stage, r, which, out_rows):
+            part = first // BANK_TILES
+            if (which, part) not in offsets:
+                offsets[(which, part)] = offsets_into_psum(which, part)
+            offset = offsets[(which, part)]
             for i in range(PAIR):
                 for h in range(HEADS):
                     nc.vector.scalar_tensor_tensor(
                         out=stage[:, h, i, :],
                         in0=stage[:, h, i, :],
                         scalar=r[:, HEADS * i + h : HEADS * i + h + 1],
-                        in1=offset[:, first + i, :],
+                        in1=offset[:, first + i - BANK_TILES * part, :],
                         op0=ALU.mult,
                         op1=ALU.add,
                     )
             nc.sync.dma_start(out=out_rows, in_=stage[:])
 
         factors = [make_factors(nc.vector, 0), make_factors(nc.vector, 1)]
-        offsets = [make_offset(nc.gpsimd, 0)]
+        make_offset(nc.gpsimd, 0)
         quantise_x(0)
-        offsets.append(make_offset(nc.vector, 1))
+        make_offset(nc.vector, 1)
         weights[0] = quantise_w(0)
         quantise_x(1)
 
@@ -253,7 +274,7 @@ def tile_groupqueryattention_pa_kernel(
                 begun = None
             else:
                 r = rotate(first, weights[g], factors[which], stage)
-                begun = (first, stage, r, offsets[which], out_rows)
+                begun = (first, stage, r, which, out_rows)
             prepare(n + LEAD)
             if waiting is not None:
                 finish(*waiting)

@@ -24,8 +24,9 @@ CHUNKS = D // 2 // P
 HEADS = 4
 COLS = HEADS * DH
 PAIR = 2
-ROUNDS_PER_GROUP = TILES // PAIR
-BANK_TILES = 512 // DH
+PAIRS = TILES // PAIR
+SHARED = 2
+LAG = 2
 LEAD = 2
 
 FLOPS = 2 * S * D * (16 + 4 + 4) * DH
@@ -38,46 +39,53 @@ def tile_groupqueryattention_pa_kernel(
     with ExitStack() as ctx:
         keep = ctx.enter_context(tc.tile_pool(name="keep", bufs=1))
         grouped_pool = ctx.enter_context(tc.tile_pool(name="grouped", bufs=2))
-        weight_pool = ctx.enter_context(tc.tile_pool(name="weights", bufs=2))
-        product_pool = ctx.enter_context(tc.tile_pool(name="products", bufs=3))
-        stage_pool = ctx.enter_context(tc.tile_pool(name="stage", bufs=4))
-        small_pool = ctx.enter_context(tc.tile_pool(name="small", bufs=4))
-        flip_psum = ctx.enter_context(tc.psum_pool(name="flip", bufs=2))
-        offset_psum = ctx.enter_context(tc.psum_pool(name="offset", bufs=2))
-        acc_psum = ctx.enter_context(tc.psum_pool(name="acc", bufs=4))
+        product_pool = ctx.enter_context(tc.tile_pool(name="products", bufs=4))
+        stage_pool = ctx.enter_context(tc.tile_pool(name="stage", bufs=6))
+        small_pool = ctx.enter_context(tc.tile_pool(name="small", bufs=6))
+        side_psum = ctx.enter_context(tc.psum_pool(name="side", bufs=4))
+        rope_psum = ctx.enter_context(tc.psum_pool(name="rope", bufs=4))
         ctx.enter_context(tc.manual_schedule())
 
         groups = [(wq[COLS * g : COLS * (g + 1), :], out_0[0, HEADS * g : HEADS * (g + 1)], 0) for g in range(4)]
         groups.append((wk, out_1[0], 1))
         groups.append((wv, out_2[0], None))
-        rounds = len(groups) * ROUNDS_PER_GROUP
+        values = len(groups) - 1
 
-        cos_sb = keep.tile([P, TILES, DH], BF16)
-        sin_sb = keep.tile([P, TILES, DH], BF16)
-        nc.scalar.dma_start(out=cos_sb[:], in_=cos_thetas.rearrange("(p t) d -> p t d", t=TILES))
-        nc.scalar.dma_start(out=sin_sb[:], in_=sin_thetas.rearrange("(p t) d -> p t d", t=TILES))
+        rounds = []
+        for g in range(values):
+            for pair in range(PAIRS):
+                rounds.append((g, pair))
+            if g < PAIRS:
+                rounds.append((values, g))
+        seen = set()
+        first_use = []
+        for g, pair in rounds:
+            fresh = [key for key in (("x", pair), ("w", g)) if key not in seen]
+            for key in fresh:
+                seen.add(key)
+            first_use.append(fresh)
+
         vectors = keep.tile([P, 4, DH], BF16)
         nc.vector.memset(vectors[:], 0.0)
         for j, vector in enumerate((q_scale, k_scale, q_shift, k_shift)):
             nc.scalar.dma_start(out=vectors[0:1, j, :], in_=vector.unsqueeze(0))
+        cos_sb = keep.tile([P, TILES, DH], BF16)
+        sin_sb = keep.tile([P, TILES, DH], BF16)
+        nc.scalar.dma_start(out=cos_sb[:], in_=cos_thetas.rearrange("(p t) d -> p t d", t=TILES))
+        nc.scalar.dma_start(out=sin_sb[:], in_=sin_thetas.rearrange("(p t) d -> p t d", t=TILES))
 
         x_sb = keep.tile([P, TILES, D], BF16)
         x_view = x[0].rearrange("(p t) d -> p t d", t=TILES)
         w_sb = [keep.tile([P, HEADS, D], BF16, name="w_sb%d" % g) for g in range(len(groups))]
-
-        def load_x(pair):
-            tiles = slice(PAIR * pair, PAIR * (pair + 1))
-            nc.sync.dma_start(out=x_sb[:, tiles, :], in_=x_view[:, tiles, :])
-
-        def load_w(g):
-            nc.sync.dma_start(out=w_sb[g][:], in_=groups[g][0].rearrange("(r p) i -> p r i", p=P))
-
-        load_x(0)
-        load_w(0)
-        for pair in range(1, ROUNDS_PER_GROUP):
-            load_x(pair)
-        for g in range(1, len(groups)):
-            load_w(g)
+        for fresh in first_use:
+            for kind, index in fresh:
+                if kind == "x":
+                    tiles = slice(PAIR * index, PAIR * (index + 1))
+                    nc.sync.dma_start(out=x_sb[:, tiles, :], in_=x_view[:, tiles, :])
+                else:
+                    w_view = groups[index][0].rearrange("(r p) i -> p r i", p=P)
+                    for r in range(HEADS):
+                        nc.sync.dma_start(out=w_sb[index][:, r, :], in_=w_view[:, r, :])
 
         ident = keep.tile([P, P], F32)
         make_identity(nc, ident[:])
@@ -86,7 +94,7 @@ def tile_groupqueryattention_pa_kernel(
         eps = keep.tile([P, 1], F32)
         nc.vector.memset(eps[:], EPS)
 
-        spread = flip_psum.tile([P, 4, DH], F32, tag="flip")
+        spread = side_psum.tile([P, 4, DH], F32, tag="side")
         nc.tensor.matmul(
             out=spread[:].rearrange("p j d -> p (j d)"),
             lhsT=ones[:],
@@ -120,75 +128,54 @@ def tile_groupqueryattention_pa_kernel(
             )
             return factors
 
-        offset_sb = keep.tile([P, 2, TILES, DH], F32)
-
         def make_offset(engine, which):
+            offset = keep.tile([P, TILES, DH], F32, name="offset%d" % which)
             turned = keep.tile([P, TILES, DH], F32, name="turned%d" % which)
-            engine.tensor_tensor(
-                out=offset_sb[:, which], in0=cos_sb[:], in1=over_tiles(shift[:, which, :], DH), op=ALU.mult
-            )
+            engine.tensor_tensor(out=offset[:], in0=cos_sb[:], in1=over_tiles(shift[:, which, :], DH), op=ALU.mult)
             engine.tensor_tensor(out=turned[:], in0=sin_sb[:], in1=over_tiles(shift_r[:, which, :], DH), op=ALU.mult)
-            engine.tensor_tensor(out=offset_sb[:, which], in0=offset_sb[:, which], in1=turned[:], op=ALU.add)
-
-        def offsets_into_psum(which, part):
-            offset = offset_psum.tile([P, BANK_TILES, DH], F32)
-            nc.tensor.matmul(
-                out=offset[:].rearrange("p t d -> p (t d)"),
-                lhsT=ident[:],
-                rhs=offset_sb[:, which, BANK_TILES * part : BANK_TILES * (part + 1), :].rearrange("p t d -> p (t d)"),
-                start=True,
-                stop=True,
-            )
+            engine.tensor_tensor(out=offset[:], in0=offset[:], in1=turned[:], op=ALU.add)
             return offset
 
         def flip_rows(rows, grouped_words):
             words = rows.bitcast(F32)
-            flipped = flip_psum.tile([P, CHUNKS, P], F32, tag="flip")
+            flipped = side_psum.tile([P, CHUNKS, P], F32, tag="side")
             for piece in range(CHUNKS):
                 nc.tensor.transpose(flipped[:, piece, :], words[:, P * piece : P * (piece + 1)], ident[:])
             nc.scalar.copy(out=grouped_words, in_=flipped[:].rearrange("p (c u) n -> p c n u", u=2))
 
         x_codes = keep.tile([P, TILES, PASSES, P], U32, align_bytes=64)
         x_scales = keep.tile([P, TILES, PASSES, P], U8, align_bytes=64)
-
-        def quantise_x(pair):
-            x_grouped = grouped_pool.tile([P, PAIR, PASSES, P, PACK], BF16, align_bytes=64)
-            for i in range(PAIR):
-                flip_rows(x_sb[:, PAIR * pair + i, :], x_grouped[:, i].bitcast(F32))
-            tiles = slice(PAIR * pair, PAIR * (pair + 1))
-            nc.vector.quantize_mx(
-                out=x_codes[:, tiles].rearrange("p t c m -> p (t c m)").bitcast(FP8X4),
-                scales=x_scales[:, tiles].rearrange("p t c m -> p (t c m)"),
-                in_=x_grouped[:].rearrange("p t c m j -> p (t c m j)"),
-            )
-
-        def quantise_w(g):
-            w_grouped = grouped_pool.tile([P, PASSES, COLS, PACK], BF16, align_bytes=64)
-            for r in range(HEADS):
-                flip_rows(w_sb[g][:, r, :], w_grouped[:, :, DH * r : DH * (r + 1), :].bitcast(F32))
-            w_codes = weight_pool.tile([P, PASSES, COLS], U32, align_bytes=64)
-            w_scales = weight_pool.tile([P, PASSES, COLS], U8, align_bytes=64)
-            nc.vector.quantize_mx(
-                out=w_codes[:].rearrange("p c n -> p (c n)").bitcast(FP8X4),
-                scales=w_scales[:].rearrange("p c n -> p (c n)"),
-                in_=w_grouped[:].rearrange("p c n j -> p (c n j)"),
-            )
-            return w_codes, w_scales
-
         weights = {}
 
-        def prepare(n):
-            g, pair = divmod(n, ROUNDS_PER_GROUP)
-            if g == 0:
-                quantise_x(pair)
-            if pair == 0 and g < len(groups):
-                weights[g] = quantise_w(g)
+        def quantise(kind, index):
+            if kind == "x":
+                x_grouped = grouped_pool.tile([P, PAIR, PASSES, P, PACK], BF16, align_bytes=64)
+                for i in range(PAIR):
+                    flip_rows(x_sb[:, PAIR * index + i, :], x_grouped[:, i].bitcast(F32))
+                tiles = slice(PAIR * index, PAIR * (index + 1))
+                nc.vector.quantize_mx(
+                    out=x_codes[:, tiles].rearrange("p t c m -> p (t c m)").bitcast(FP8X4),
+                    scales=x_scales[:, tiles].rearrange("p t c m -> p (t c m)"),
+                    in_=x_grouped[:].rearrange("p t c m j -> p (t c m j)"),
+                )
+            else:
+                w_grouped = grouped_pool.tile([P, PASSES, COLS, PACK], BF16, align_bytes=64)
+                for r in range(HEADS):
+                    flip_rows(w_sb[index][:, r, :], w_grouped[:, :, DH * r : DH * (r + 1), :].bitcast(F32))
+                w_codes = keep.tile([P, PASSES, COLS], U32, align_bytes=64, name="w_codes%d" % index)
+                w_scales = keep.tile([P, PASSES, COLS], U8, align_bytes=64, name="w_scales%d" % index)
+                nc.vector.quantize_mx(
+                    out=w_codes[:].rearrange("p c n -> p (c n)").bitcast(FP8X4),
+                    scales=w_scales[:].rearrange("p c n -> p (c n)"),
+                    in_=w_grouped[:].rearrange("p c n j -> p (c n j)"),
+                )
+                weights[index] = (w_codes, w_scales)
 
-        def project(t, w_codes, w_scales):
-            acc = acc_psum.tile([P, COLS], F32)
+        def project(acc, t, g):
+            w_codes, w_scales = weights[g]
             for c in range(PASSES):
                 nc.tensor.matmul_mx(
-                    out=acc[:],
+                    out=acc,
                     lhsT=x_codes[:, t, c, :].bitcast(FP8X4),
                     lhsT_scale=x_scales[:, t, c, :],
                     rhs=w_codes[:, c, :].bitcast(FP8X4),
@@ -196,86 +183,92 @@ def tile_groupqueryattention_pa_kernel(
                     start=(c == 0),
                     stop=(c == PASSES - 1),
                 )
-            return acc
 
         squares = keep.tile([P, DH], F32)
 
-        def rotate(first, w_pair, factors, stage):
-            products = product_pool.tile([P, PAIR, 2, COLS], F32)
-            sum_sq = small_pool.tile([P, PAIR * HEADS], F32)
+        def rotate(first, g, factors, stage):
+            products = product_pool.tile([P, 2, HEADS, PAIR, DH], F32)
+            sum_sq = small_pool.tile([P, HEADS, PAIR], F32)
             for i in range(PAIR):
-                acc = project(first + i, *w_pair)
+                acc = rope_psum.tile([P, COLS], F32)
+                project(acc[:], first + i, g)
                 for h in range(HEADS):
                     nc.scalar.activation(
                         out=squares[:],
                         in_=acc[:, DH * h : DH * (h + 1)],
                         func=ACT.Square,
-                        accum_out=sum_sq[:, HEADS * i + h : HEADS * i + h + 1],
+                        accum_out=sum_sq[:, h, i : i + 1],
                     )
                 nc.vector.tensor_tensor(
-                    out=products[:, i].rearrange("p j (h d) -> p j h d", d=DH),
+                    out=products[:, :, :, i, :],
                     in0=acc[:].rearrange("p (h d) -> p h d", d=DH).unsqueeze(1).to_broadcast([P, 2, HEADS, DH]),
                     in1=factors[:, first + i].unsqueeze(2).to_broadcast([P, 2, HEADS, DH]),
                     op=ALU.mult,
                 )
-            rms = small_pool.tile([P, PAIR * HEADS], F32)
-            nc.scalar.activation(out=rms[:], in_=sum_sq[:], func=ACT.Sqrt, scale=1.0 / DH, bias=eps[:, 0:1])
-            r = small_pool.tile([P, PAIR * HEADS], F32)
-            nc.vector.reciprocal(out=r[:], in_=rms[:])
-            straight = products[:, :, 0, :].rearrange("p i (h d) -> p i h d", d=DH)
-            crossed = products[:, :, 1, :].rearrange("p i (h d) -> p i h d", d=DH)
-            rotated = stage[:].rearrange("p h i d -> p i h d")
-            nc.gpsimd.tensor_tensor(
-                out=rotated[:, :, :, low], in0=straight[:, :, :, low], in1=crossed[:, :, :, high], op=ALU.add
+            r = small_pool.tile([P, HEADS, PAIR], F32)
+            nc.scalar.activation(
+                out=r[:], in_=sum_sq[:], func=ACT.Abs_reciprocal_sqrt, scale=1.0 / DH, bias=eps[:, 0:1]
             )
             nc.gpsimd.tensor_tensor(
-                out=rotated[:, :, :, high], in0=straight[:, :, :, high], in1=crossed[:, :, :, low], op=ALU.add
+                out=stage[:].rearrange("p h i (f e) -> p (h i) f e", f=2),
+                in0=products[:, 0].rearrange("p h i (f e) -> p (h i) f e", f=2),
+                in1=products[:, 1].rearrange("p h i (f e) -> p (h i) f e", f=2)[:, :, ::-1, :],
+                op=ALU.add,
             )
             return r
 
-        offsets = {}
-
-        def finish(first, stage, r, which, out_rows):
-            part = first // BANK_TILES
-            if (which, part) not in offsets:
-                offsets[(which, part)] = offsets_into_psum(which, part)
-            offset = offsets[(which, part)]
-            for i in range(PAIR):
-                for h in range(HEADS):
-                    nc.vector.scalar_tensor_tensor(
-                        out=stage[:, h, i, :],
-                        in0=stage[:, h, i, :],
-                        scalar=r[:, HEADS * i + h : HEADS * i + h + 1],
-                        in1=offset[:, first + i - BANK_TILES * part, :],
-                        op0=ALU.mult,
-                        op1=ALU.add,
-                    )
+        def finish(first, stage, r, offset, out_rows):
+            for h in range(HEADS):
+                for i in range(PAIR):
+                    if h < HEADS - SHARED:
+                        nc.vector.scalar_tensor_tensor(
+                            out=stage[:, h, i, :],
+                            in0=stage[:, h, i, :],
+                            scalar=r[:, h, i : i + 1],
+                            in1=offset[:, first + i, :],
+                            op0=ALU.mult,
+                            op1=ALU.add,
+                        )
+                    else:
+                        nc.scalar.activation(
+                            out=stage[:, h, i, :], in_=stage[:, h, i, :], func=ACT.Copy, scale=r[:, h, i : i + 1]
+                        )
+            nc.gpsimd.tensor_tensor(
+                out=stage[:, HEADS - SHARED : HEADS],
+                in0=stage[:, HEADS - SHARED : HEADS],
+                in1=offset[:, first : first + PAIR, :].unsqueeze(1).to_broadcast([P, SHARED, PAIR, DH]),
+                op=ALU.add,
+            )
             nc.sync.dma_start(out=out_rows, in_=stage[:])
 
-        factors = [make_factors(nc.vector, 0), make_factors(nc.vector, 1)]
-        make_offset(nc.gpsimd, 0)
-        quantise_x(0)
-        make_offset(nc.vector, 1)
-        weights[0] = quantise_w(0)
-        quantise_x(1)
+        factors = [make_factors(nc.vector, 0)]
+        offsets = [make_offset(nc.gpsimd, 0)]
+        quantise("x", 0)
+        factors.append(make_factors(nc.vector, 1))
+        quantise("w", 0)
+        quantise("x", 1)
+        offsets.append(make_offset(nc.vector, 1))
 
-        waiting = None
-        for n in range(rounds):
-            g, pair = divmod(n, ROUNDS_PER_GROUP)
+        waiting = []
+        for n, (g, pair) in enumerate(rounds):
             first = PAIR * pair
             which = groups[g][2]
             out_rows = groups[g][1].rearrange("h (p t) d -> p h t d", t=TILES)[:, :, first : first + PAIR, :]
             stage = stage_pool.tile([P, HEADS, PAIR, DH], F32)
             if which is None:
                 for i in range(PAIR):
-                    acc = project(first + i, *weights[g])
+                    acc = side_psum.tile([P, COLS], F32, tag="side")
+                    project(acc[:], first + i, g)
                     nc.scalar.copy(out=stage[:, :, i, :], in_=acc[:].rearrange("p (h d) -> p h d", d=DH))
                 nc.sync.dma_start(out=out_rows, in_=stage[:])
-                begun = None
             else:
-                r = rotate(first, weights[g], factors[which], stage)
-                begun = (first, stage, r, which, out_rows)
-            prepare(n + LEAD)
-            if waiting is not None:
-                finish(*waiting)
-            waiting = begun
+                r = rotate(first, g, factors[which], stage)
+            if n + LEAD < len(rounds):
+                for kind, index in first_use[n + LEAD]:
+                    quantise(kind, index)
+            if which is not None:
+                waiting.append((first, stage, r, offsets[which], out_rows))
+                if len(waiting) > LAG:
+                    finish(*waiting.pop(0))
+        for begun in waiting:
+            finish(*begun)

from contextlib import ExitStack

import concourse.mybir as mybir
from concourse.masks import make_identity

F32 = mybir.dt.float32
BF16 = mybir.dt.bfloat16
U32 = mybir.dt.uint32
U8 = mybir.dt.uint8
FP8X4 = mybir.dt.float8_e4m3fn_x4
ALU = mybir.AluOpType
ACT = mybir.ActivationFunctionType

P = 128
S = 1024
D = 1024
DH = 128
HALF = DH // 2
EPS = 1e-6
TILES = S // P
PACK = 4
PASSES = D // (P * PACK)
CHUNKS = D // 2 // P
HEADS = 4
COLS = HEADS * DH
PAIR = 2
PAIRS = TILES // PAIR
SHARED = 2
LAG = 2
LEAD = 2

FLOPS = 2 * S * D * (16 + 4 + 4) * DH


def tile_groupqueryattention_pa_kernel(
    tc, x, sin_thetas, cos_thetas, wq, wk, wv, q_scale, q_shift, k_scale, k_shift, out_0, out_1, out_2
):
    nc = tc.nc
    with ExitStack() as ctx:
        keep = ctx.enter_context(tc.tile_pool(name="keep", bufs=1))
        grouped_pool = ctx.enter_context(tc.tile_pool(name="grouped", bufs=2))
        product_pool = ctx.enter_context(tc.tile_pool(name="products", bufs=4))
        stage_pool = ctx.enter_context(tc.tile_pool(name="stage", bufs=6))
        small_pool = ctx.enter_context(tc.tile_pool(name="small", bufs=6))
        side_psum = ctx.enter_context(tc.psum_pool(name="side", bufs=4))
        rope_psum = ctx.enter_context(tc.psum_pool(name="rope", bufs=4))
        ctx.enter_context(tc.manual_schedule())

        groups = [(wq[COLS * g : COLS * (g + 1), :], out_0[0, HEADS * g : HEADS * (g + 1)], 0) for g in range(4)]
        groups.append((wk, out_1[0], 1))
        groups.append((wv, out_2[0], None))
        values = len(groups) - 1

        rounds = []
        for g in range(values):
            for pair in range(PAIRS):
                rounds.append((g, pair))
            if g < PAIRS:
                rounds.append((values, g))
        seen = set()
        first_use = []
        for g, pair in rounds:
            fresh = [key for key in (("x", pair), ("w", g)) if key not in seen]
            for key in fresh:
                seen.add(key)
            first_use.append(fresh)

        vectors = keep.tile([P, 4, DH], BF16)
        nc.vector.memset(vectors[:], 0.0)
        for j, vector in enumerate((q_scale, k_scale, q_shift, k_shift)):
            nc.scalar.dma_start(out=vectors[0:1, j, :], in_=vector.unsqueeze(0))
        cos_sb = keep.tile([P, TILES, DH], BF16)
        sin_sb = keep.tile([P, TILES, DH], BF16)
        nc.scalar.dma_start(out=cos_sb[:], in_=cos_thetas.rearrange("(p t) d -> p t d", t=TILES))
        nc.scalar.dma_start(out=sin_sb[:], in_=sin_thetas.rearrange("(p t) d -> p t d", t=TILES))

        x_sb = keep.tile([P, TILES, D], BF16)
        x_view = x[0].rearrange("(p t) d -> p t d", t=TILES)
        w_sb = [keep.tile([P, HEADS, D], BF16, name="w_sb%d" % g) for g in range(len(groups))]
        for fresh in first_use:
            for kind, index in fresh:
                if kind == "x":
                    tiles = slice(PAIR * index, PAIR * (index + 1))
                    nc.sync.dma_start(out=x_sb[:, tiles, :], in_=x_view[:, tiles, :])
                else:
                    w_view = groups[index][0].rearrange("(r p) i -> p r i", p=P)
                    for r in range(HEADS):
                        nc.sync.dma_start(out=w_sb[index][:, r, :], in_=w_view[:, r, :])

        ident = keep.tile([P, P], F32)
        make_identity(nc, ident[:])
        ones = keep.tile([P, P], BF16)
        nc.vector.memset(ones[:], 1.0)
        eps = keep.tile([P, 1], F32)
        nc.vector.memset(eps[:], EPS)

        spread = side_psum.tile([P, 4, DH], F32, tag="side")
        nc.tensor.matmul(
            out=spread[:].rearrange("p j d -> p (j d)"),
            lhsT=ones[:],
            rhs=vectors[:].rearrange("p j d -> p (j d)"),
            start=True,
            stop=True,
        )
        low, high = slice(0, HALF), slice(HALF, DH)
        gain = keep.tile([P, 2, DH], F32)
        gain_s = keep.tile([P, 2, DH], F32)
        shift = keep.tile([P, 2, DH], F32)
        shift_r = keep.tile([P, 2, DH], F32)
        nc.vector.tensor_scalar_add(out=gain[:], in0=spread[:, 0:2, :], scalar1=1.0)
        nc.vector.tensor_copy(out=gain_s[:, :, low], in_=gain[:, :, low])
        nc.vector.tensor_scalar_mul(out=gain_s[:, :, high], in0=gain[:, :, high], scalar1=-1.0)
        nc.vector.tensor_copy(out=shift[:], in_=spread[:, 2:4, :])
        nc.vector.tensor_scalar_mul(out=shift_r[:, :, low], in0=spread[:, 2:4, high], scalar1=-1.0)
        nc.vector.tensor_copy(out=shift_r[:, :, high], in_=spread[:, 2:4, low])

        def over_tiles(vector, width):
            return vector.unsqueeze(1).to_broadcast([P, TILES, width])

        def make_factors(engine, which):
            factors = keep.tile([P, TILES, 2, DH], F32, name="factors%d" % which)
            engine.tensor_tensor(out=factors[:, :, 0, :], in0=cos_sb[:], in1=over_tiles(gain[:, which, :], DH), op=ALU.mult)
            engine.tensor_tensor(
                out=factors[:, :, 1, low], in0=sin_sb[:, :, high], in1=over_tiles(gain_s[:, which, low], HALF), op=ALU.mult
            )
            engine.tensor_tensor(
                out=factors[:, :, 1, high], in0=sin_sb[:, :, low], in1=over_tiles(gain_s[:, which, high], HALF), op=ALU.mult
            )
            return factors

        def make_offset(engine, which):
            offset = keep.tile([P, TILES, DH], F32, name="offset%d" % which)
            turned = keep.tile([P, TILES, DH], F32, name="turned%d" % which)
            engine.tensor_tensor(out=offset[:], in0=cos_sb[:], in1=over_tiles(shift[:, which, :], DH), op=ALU.mult)
            engine.tensor_tensor(out=turned[:], in0=sin_sb[:], in1=over_tiles(shift_r[:, which, :], DH), op=ALU.mult)
            engine.tensor_tensor(out=offset[:], in0=offset[:], in1=turned[:], op=ALU.add)
            return offset

        def flip_rows(rows, grouped_words):
            words = rows.bitcast(F32)
            flipped = side_psum.tile([P, CHUNKS, P], F32, tag="side")
            for piece in range(CHUNKS):
                nc.tensor.transpose(flipped[:, piece, :], words[:, P * piece : P * (piece + 1)], ident[:])
            nc.scalar.copy(out=grouped_words, in_=flipped[:].rearrange("p (c u) n -> p c n u", u=2))

        x_codes = keep.tile([P, TILES, PASSES, P], U32, align_bytes=64)
        x_scales = keep.tile([P, TILES, PASSES, P], U8, align_bytes=64)
        weights = {}

        def quantise(kind, index):
            if kind == "x":
                x_grouped = grouped_pool.tile([P, PAIR, PASSES, P, PACK], BF16, align_bytes=64)
                for i in range(PAIR):
                    flip_rows(x_sb[:, PAIR * index + i, :], x_grouped[:, i].bitcast(F32))
                tiles = slice(PAIR * index, PAIR * (index + 1))
                nc.vector.quantize_mx(
                    out=x_codes[:, tiles].rearrange("p t c m -> p (t c m)").bitcast(FP8X4),
                    scales=x_scales[:, tiles].rearrange("p t c m -> p (t c m)"),
                    in_=x_grouped[:].rearrange("p t c m j -> p (t c m j)"),
                )
            else:
                w_grouped = grouped_pool.tile([P, PASSES, COLS, PACK], BF16, align_bytes=64)
                for r in range(HEADS):
                    flip_rows(w_sb[index][:, r, :], w_grouped[:, :, DH * r : DH * (r + 1), :].bitcast(F32))
                w_codes = keep.tile([P, PASSES, COLS], U32, align_bytes=64, name="w_codes%d" % index)
                w_scales = keep.tile([P, PASSES, COLS], U8, align_bytes=64, name="w_scales%d" % index)
                nc.vector.quantize_mx(
                    out=w_codes[:].rearrange("p c n -> p (c n)").bitcast(FP8X4),
                    scales=w_scales[:].rearrange("p c n -> p (c n)"),
                    in_=w_grouped[:].rearrange("p c n j -> p (c n j)"),
                )
                weights[index] = (w_codes, w_scales)

        def project(acc, t, g):
            w_codes, w_scales = weights[g]
            for c in range(PASSES):
                nc.tensor.matmul_mx(
                    out=acc,
                    lhsT=x_codes[:, t, c, :].bitcast(FP8X4),
                    lhsT_scale=x_scales[:, t, c, :],
                    rhs=w_codes[:, c, :].bitcast(FP8X4),
                    rhs_scale=w_scales[:, c, :],
                    start=(c == 0),
                    stop=(c == PASSES - 1),
                )

        squares = keep.tile([P, DH], F32)

        def rotate(first, g, factors, stage):
            products = product_pool.tile([P, 2, HEADS, PAIR, DH], F32)
            sum_sq = small_pool.tile([P, HEADS, PAIR], F32)
            for i in range(PAIR):
                acc = rope_psum.tile([P, COLS], F32)
                project(acc[:], first + i, g)
                for h in range(HEADS):
                    nc.scalar.activation(
                        out=squares[:],
                        in_=acc[:, DH * h : DH * (h + 1)],
                        func=ACT.Square,
                        accum_out=sum_sq[:, h, i : i + 1],
                    )
                nc.vector.tensor_tensor(
                    out=products[:, :, :, i, :],
                    in0=acc[:].rearrange("p (h d) -> p h d", d=DH).unsqueeze(1).to_broadcast([P, 2, HEADS, DH]),
                    in1=factors[:, first + i].unsqueeze(2).to_broadcast([P, 2, HEADS, DH]),
                    op=ALU.mult,
                )
            r = small_pool.tile([P, HEADS, PAIR], F32)
            nc.scalar.activation(
                out=r[:], in_=sum_sq[:], func=ACT.Abs_reciprocal_sqrt, scale=1.0 / DH, bias=eps[:, 0:1]
            )
            nc.gpsimd.tensor_tensor(
                out=stage[:].rearrange("p h i (f e) -> p (h i) f e", f=2),
                in0=products[:, 0].rearrange("p h i (f e) -> p (h i) f e", f=2),
                in1=products[:, 1].rearrange("p h i (f e) -> p (h i) f e", f=2)[:, :, ::-1, :],
                op=ALU.add,
            )
            return r

        def finish(first, stage, r, offset, out_rows):
            for h in range(HEADS):
                for i in range(PAIR):
                    if h < HEADS - SHARED:
                        nc.vector.scalar_tensor_tensor(
                            out=stage[:, h, i, :],
                            in0=stage[:, h, i, :],
                            scalar=r[:, h, i : i + 1],
                            in1=offset[:, first + i, :],
                            op0=ALU.mult,
                            op1=ALU.add,
                        )
                    else:
                        nc.scalar.activation(
                            out=stage[:, h, i, :], in_=stage[:, h, i, :], func=ACT.Copy, scale=r[:, h, i : i + 1]
                        )
            nc.gpsimd.tensor_tensor(
                out=stage[:, HEADS - SHARED : HEADS],
                in0=stage[:, HEADS - SHARED : HEADS],
                in1=offset[:, first : first + PAIR, :].unsqueeze(1).to_broadcast([P, SHARED, PAIR, DH]),
                op=ALU.add,
            )
            nc.sync.dma_start(out=out_rows, in_=stage[:])

        factors = [make_factors(nc.vector, 0)]
        offsets = [make_offset(nc.gpsimd, 0)]
        quantise("x", 0)
        factors.append(make_factors(nc.vector, 1))
        quantise("w", 0)
        quantise("x", 1)
        offsets.append(make_offset(nc.vector, 1))

        waiting = []
        for n, (g, pair) in enumerate(rounds):
            first = PAIR * pair
            which = groups[g][2]
            out_rows = groups[g][1].rearrange("h (p t) d -> p h t d", t=TILES)[:, :, first : first + PAIR, :]
            stage = stage_pool.tile([P, HEADS, PAIR, DH], F32)
            if which is None:
                for i in range(PAIR):
                    acc = side_psum.tile([P, COLS], F32, tag="side")
                    project(acc[:], first + i, g)
                    nc.scalar.copy(out=stage[:, :, i, :], in_=acc[:].rearrange("p (h d) -> p h d", d=DH))
                nc.sync.dma_start(out=out_rows, in_=stage[:])
            else:
                r = rotate(first, g, factors[which], stage)
            if n + LEAD < len(rounds):
                for kind, index in first_use[n + LEAD]:
                    quantise(kind, index)
            if which is not None:
                waiting.append((first, stage, r, offsets[which], out_rows))
                if len(waiting) > LAG:
                    finish(*waiting.pop(0))
        for begun in waiting:
            finish(*begun)
